import numpy as np
import ml_dtypes


BF16 = ml_dtypes.bfloat16


def bf(x):
    return np.asarray(x, np.float32).astype(BF16)


def f64(x):
    return np.asarray(x).astype(np.float64)


E2M1 = np.array([0.0, 0.5, 1.0, 1.5, 2.0, 3.0, 4.0, 6.0, -0.0, -0.5, -1.0, -1.5, -2.0, -3.0, -4.0, -6.0])


def pack_weight(w, fmt):
    k, n = w.shape
    w = f64(bf(w)).reshape(k // 32, 32, n)
    amax = np.abs(w).max(1)
    if fmt == "e4m3":
        byte = np.frexp(amax)[1] - 1 + 127 - 7
    else:
        mant, ex = np.frexp(amax / 6.0)
        byte = np.where(mant > 0.5, ex, ex - 1) + 127
    byte = np.clip(np.where(amax > 0, byte, 1), 1, 254)
    scaled = (w * np.exp2(127.0 - byte)[:, None, :]).reshape(k, n).astype(np.float32)
    by_word = np.ascontiguousarray(scaled.reshape(k // 512, 128, 4, n).transpose(0, 1, 3, 2))
    if fmt == "e4m3":
        words = by_word.astype(ml_dtypes.float8_e4m3fn).view(np.uint8)
    else:
        c = by_word.astype(ml_dtypes.float4_e2m1fn).view(np.uint8) & 0xF
        words = c[..., 0::2] | (c[..., 1::2] << 4)
    return np.ascontiguousarray(words), np.ascontiguousarray(byte.astype(np.uint8).reshape(k // 512, 16, n))


def unpack_weight(words, scales, fmt):
    g, p, n, _ = words.shape
    if fmt == "e4m3":
        vals = np.ascontiguousarray(words).view(ml_dtypes.float8_e4m3fn).astype(np.float64)
    else:
        nib = np.empty((g, p, n, 4), np.uint8)
        nib[..., 0::2] = words & 0xF
        nib[..., 1::2] = words >> 4
        vals = E2M1[nib]
    vals = vals * np.repeat(np.exp2(scales.astype(np.float64) - 127.0), 8, axis=1)[..., None]
    return vals.transpose(0, 1, 3, 2).reshape(g * 512, n)

def pack4(w):
    words, scales = pack_weight(w, "e2m1")
    return words.reshape(words.shape[0], 128, -1), scales


def unpack4(words, scales):
    return unpack_weight(words.reshape(words.shape[0], 128, -1, 2), scales, "e2m1")


def kspread(k):
    return np.exp2(np.repeat(np.random.randint(-6, 7, k // 32), 32).astype(np.float64))


N, N_CH, X, H = 128, 5, 1024, 1024
K = N_CH * H


def sigmoid(v):
    return 1.0 / (1.0 + np.exp(-v))


def setup_inputs():
    s, t = kspread(X), kspread(K)
    x = np.random.standard_normal((N, X)) * s
    x_words, x_scales = pack4(np.ascontiguousarray(x.T))
    x_mask = bf(np.random.random(N) < 0.75)
    neighbour_h = np.random.standard_normal((N, N_CH, H)) * t.reshape(N_CH, H)
    neighbour_h_words, neighbour_h_scales = pack4(np.ascontiguousarray(neighbour_h.reshape(N, K).T))
    neighbour_c = bf(np.random.standard_normal((N, N_CH, H)))
    W_f_in_words, W_f_in_scales = pack4(np.random.standard_normal((X, H)) * 0.5 / np.sqrt(X) / s[:, None])
    b_f_in = bf(np.random.standard_normal(H) * 0.3)
    W_aggr_f_words, W_aggr_f_scales = pack4(np.random.standard_normal((K, K)) / np.sqrt(K) / t[:, None])
    b_aggr_f = bf(np.random.standard_normal(K) * 0.3)
    return {
        "x_words": x_words,
        "x_scales": x_scales,
        "x_mask": x_mask,
        "neighbour_h_words": neighbour_h_words,
        "neighbour_h_scales": neighbour_h_scales,
        "neighbour_c": neighbour_c,
        "W_f_in_words": W_f_in_words,
        "W_f_in_scales": W_f_in_scales,
        "b_f_in": b_f_in,
        "W_aggr_f_words": W_aggr_f_words,
        "W_aggr_f_scales": W_aggr_f_scales,
        "b_aggr_f": b_aggr_f,
    }


def reference(x_words, x_scales, x_mask, neighbour_h_words, neighbour_h_scales, neighbour_c, W_f_in_words, W_f_in_scales, b_f_in, W_aggr_f_words, W_aggr_f_scales, b_aggr_f):
    h_flat = unpack4(neighbour_h_words, neighbour_h_scales).T
    f_input = ((unpack4(x_words, x_scales).T @ unpack4(W_f_in_words, W_f_in_scales)) + f64(b_f_in)) * f64(x_mask)[:, None]
    f_input = np.tile(f_input, (1, N_CH))
    f_gate = (h_flat @ unpack4(W_aggr_f_words, W_aggr_f_scales)) + f64(b_aggr_f) + f_input
    f_aggr = f_gate + f_input
    f = sigmoid(f_aggr).reshape(N, N_CH, H)
    return np.sum(f * f64(neighbour_c), axis=1)

@@ -1,0 +1,291 @@
+from contextlib import ExitStack
+
+import concourse.mybir as mybir
+from concourse.masks import make_identity
+
+N, N_CH, X, H = 128, 5, 1024, 1024
+K = N_CH * H
+FLOPS = 2 * N * (K * K + X * H)
+
+P = 128
+BLK = 512
+K_PASS = 512
+G_H = K // K_PASS
+G_X = X // K_PASS
+HALVES = H // BLK
+N_BLK = K // BLK
+SWEEPS = (6, 3, 1)
+PLANE_CUTS = ((0, 2, 5, 10), (0, 10), (0, 10))
+
+F32 = mybir.dt.float32
+BF16 = mybir.dt.bfloat16
+I32 = mybir.dt.int32
+U8 = mybir.dt.uint8
+FP4X4 = mybir.dt.float4_e2m1fn_x4
+ACT = mybir.ActivationFunctionType
+ALU = mybir.AluOpType
+
+
+def tile_treelstmcell_pa_kernel(
+    tc,
+    x_words,
+    x_scales,
+    x_mask,
+    neighbour_h_words,
+    neighbour_h_scales,
+    neighbour_c,
+    W_f_in_words,
+    W_f_in_scales,
+    b_f_in,
+    W_aggr_f_words,
+    W_aggr_f_scales,
+    b_aggr_f,
+    out,
+):
+    nc = tc.nc
+    with ExitStack() as ctx:
+        keep = ctx.enter_context(tc.tile_pool(name="keep", bufs=1))
+        work = ctx.enter_context(tc.tile_pool(name="work", bufs=3))
+        psum = ctx.enter_context(tc.psum_pool(name="psum", bufs=1))
+        ctx.enter_context(tc.manual_schedule())
+
+        def codes_tile(name, passes, cols):
+            return keep.tile([P, passes, 2 * cols], U8, name=name, align_bytes=64)
+
+        def plane_tile(name, passes, cols):
+            return keep.tile([P, passes, cols], U8, name=name, align_bytes=64)
+
+        def bank(i, name):
+            return psum.tile([P, BLK], F32, name=name, tag="bank%d" % i)
+
+        hf_codes = codes_tile("hf_codes", G_H, N)
+        hf_plane = plane_tile("hf_plane", G_H, N)
+        x_codes = codes_tile("x_codes", G_X, N)
+        x_plane = plane_tile("x_plane", G_X, N)
+        wf_codes = codes_tile("wf_codes", G_X, H)
+        wf_plane = plane_tile("wf_plane", G_X, H)
+        w_codes = [codes_tile("w_codes%d" % s, G_H, BLK * n) for s, n in enumerate(SWEEPS)]
+        w_plane = [
+            [(g0, g1, plane_tile("w_plane%d_%d" % (s, g0), g1 - g0, BLK * n)) for g0, g1 in zip(cuts, cuts[1:])]
+            for s, (n, cuts) in enumerate(zip(SWEEPS, PLANE_CUTS))
+        ]
+        sweep_col = [BLK * sum(SWEEPS[:s]) for s in range(len(SWEEPS))]
+
+        warm = keep.tile([P, 1], F32, name="warm")
+        nc.gpsimd.memset(warm[:], 0.0)
+        nc.scalar.activation(out=warm[:], in_=warm[:], func=ACT.Sigmoid)
+        rows = keep.tile([P, BLK], BF16, name="rows")
+        nc.gpsimd.memset(rows[:], 0.0)
+        ident = keep.tile([P, P], BF16, name="ident")
+        make_identity(nc, ident[:])
+        nc.gpsimd.dma_start(out=rows[0:N_BLK, :], in_=b_aggr_f.rearrange("(j n) -> j n", n=BLK))
+        nc.gpsimd.dma_start(out=rows[N_BLK : N_BLK + HALVES, :], in_=b_f_in.rearrange("(j n) -> j n", n=BLK))
+        nc.gpsimd.dma_start(out=rows[N_BLK + HALVES : N_BLK + HALVES + 1, 0:N], in_=x_mask.unsqueeze(0))
+
+        def zero(plane):
+            nc.vector.memset(plane[:].rearrange("p g n -> p (g n)").bitcast(I32), 0)
+
+        def load_codes(tile, words, g0, g1, c0, cols):
+            nc.sync.dma_start(
+                out=tile[:, g0:g1, :].bitcast(I32),
+                in_=words[g0:g1, :, 2 * c0 : 2 * (c0 + cols)].rearrange("g p c -> p g c").bitcast(I32),
+            )
+
+        def rows_by_r(tile, scales, g0, g1, c0, cols, r):
+            nc.sync.dma_start(
+                out=tile[r:P:32, :, :].bitcast(I32),
+                in_=scales[g0:g1, r:16:4, c0 : c0 + cols].rearrange("g q n -> q g n").bitcast(I32),
+            )
+
+        def w_load(s, g0, g1):
+            load_codes(w_codes[s], W_aggr_f_words, g0, g1, sweep_col[s], BLK * SWEEPS[s])
+
+        def w_scale(s, i, r):
+            g0, g1, plane = w_plane[s][i]
+            rows_by_r(plane, W_aggr_f_scales, g0, g1, sweep_col[s], BLK * SWEEPS[s], r)
+
+        zero(hf_plane)
+        for g0, g1, plane in w_plane[0]:
+            zero(plane)
+        zero(x_plane)
+        zero(wf_plane)
+        zero(w_plane[1][0][2])
+        zero(w_plane[2][0][2])
+
+        def rows_of_quadrant(tile, scales, g0, g1, c0, cols, q):
+            nc.sync.dma_start(
+                out=tile[32 * q : 32 * q + 4, :, :].bitcast(I32),
+                in_=scales[g0:g1, 4 * q : 4 * q + 4, c0 : c0 + cols].rearrange("g q n -> q g n").bitcast(I32),
+            )
+
+        def x_rows(q):
+            rows_of_quadrant(x_plane, x_scales, 0, G_X, 0, N, q)
+
+        def wf_rows(q):
+            rows_of_quadrant(wf_plane, W_f_in_scales, 0, G_X, 0, H, q)
+
+        w_load(0, 0, 1)
+        load_codes(hf_codes, neighbour_h_words, 0, G_H, 0, N)
+        for q in range(4):
+            rows_of_quadrant(hf_plane, neighbour_h_scales, 0, G_H, 0, N, q)
+        for q in range(4):
+            rows_of_quadrant(w_plane[0][0][2], W_aggr_f_scales, 0, 2, 0, BLK * SWEEPS[0], q)
+        w_load(0, 1, 2)
+        w_scale(0, 1, 0)
+        w_load(0, 2, 3)
+        w_scale(0, 1, 1)
+        w_load(0, 3, 4)
+        w_scale(0, 1, 2)
+        w_load(0, 4, 5)
+        w_scale(0, 1, 3)
+        load_codes(x_codes, x_words, 0, G_X, 0, N)
+        load_codes(wf_codes, W_f_in_words, 0, G_X, 0, H)
+        x_rows(0)
+        x_rows(1)
+        w_load(0, 5, 6)
+        w_scale(0, 2, 0)
+        x_rows(2)
+        x_rows(3)
+        w_load(0, 6, 7)
+        w_scale(0, 2, 1)
+        wf_rows(0)
+        wf_rows(1)
+        w_load(0, 7, 8)
+        w_scale(0, 2, 2)
+        wf_rows(2)
+        wf_rows(3)
+        w_load(0, 8, 9)
+        w_scale(0, 2, 3)
+        c_in = keep.tile([P, K], BF16, name="c_in")
+        nc.sync.dma_start(out=c_in[:], in_=neighbour_c.rearrange("n c h -> n (c h)"))
+        w_scale(1, 0, 0)
+        w_load(0, 9, 10)
+        w_scale(1, 0, 1)
+        w_load(1, 0, 2)
+        w_scale(1, 0, 2)
+        w_load(1, 2, 4)
+        w_scale(1, 0, 3)
+        w_load(1, 4, 6)
+        w_scale(2, 0, 0)
+        w_load(1, 6, 8)
+        w_scale(2, 0, 1)
+        w_load(1, 8, 10)
+        w_scale(2, 0, 2)
+        w_load(2, 0, 5)
+        w_scale(2, 0, 3)
+        w_load(2, 5, 8)
+        w_load(2, 8, 9)
+        w_load(2, 9, 10)
+
+        def mx(acc, a_codes, a_plane, b_codes, b_plane, b_g, g, n0, first, last):
+            nc.tensor.matmul_mx(
+                out=acc[:],
+                lhsT=a_codes[:, g, :].bitcast(FP4X4),
+                lhsT_scale=a_plane[:, g, :],
+                rhs=b_codes[:, g, 2 * n0 : 2 * (n0 + BLK)].bitcast(FP4X4),
+                rhs_scale=b_plane[:, b_g, n0 : n0 + BLK],
+                start=first,
+                stop=last,
+            )
+
+        def w_pass(s, g, i, acc):
+            for g0, g1, plane in w_plane[s]:
+                if g0 <= g < g1:
+                    mx(acc, hf_codes, hf_plane, w_codes[s], plane, g - g0, g, BLK * i, g == 0, g == G_H - 1)
+
+        def sweep(s, accs, g0, g1, i0=0):
+            for g in range(g0, g1):
+                for i, acc in enumerate(accs):
+                    w_pass(s, g, i0 + i, acc)
+
+        mask2 = keep.tile([P, 1], F32, name="mask2")
+        fin = [keep.tile([P, BLK], F32, name="fin%d" % h) for h in range(HALVES)]
+        add = [keep.tile([P, BLK], F32, name="add%d" % j) for j in range(N_BLK)]
+
+        def spread(j, b):
+            acc = bank(b, "bias_ps%d" % j)
+            nc.tensor.matmul(out=acc[:], lhsT=ident[:, j : j + 1].to_broadcast([P, P]), rhs=rows[:], start=True, stop=True)
+            if j < N_BLK:
+                nc.scalar.copy(out=add[j][:], in_=acc[:])
+            else:
+                nc.scalar.activation(out=fin[j - N_BLK][:], in_=acc[:], func=ACT.Copy, scale=mask2[:, 0:1])
+
+        def spread_mask():
+            mask_ps = bank(6, "mask_ps")
+            nc.tensor.matmul(
+                out=mask_ps[:, 0:1], lhsT=rows[:, 0:N], rhs=ident[:, N_BLK + HALVES : N_BLK + HALVES + 1], start=True, stop=True
+            )
+            nc.scalar.mul(mask2[:], mask_ps[:, 0:1], 2.0)
+
+        acc_a = [bank(i, "acc_a%d" % i) for i in range(SWEEPS[0])]
+        sweep(0, acc_a, 0, 1)
+        spread_mask()
+        spread(N_BLK, 7)
+        sweep(0, acc_a[0:3], 1, 2)
+        spread(N_BLK + 1, 6)
+        sweep(0, acc_a[3:], 1, 2, 3)
+        for g in range(2, 7):
+            sweep(0, acc_a[0:3], g, g + 1)
+            spread(2 * (g - 2), 7)
+            sweep(0, acc_a[3:], g, g + 1, 3)
+            spread(2 * (g - 2) + 1, 6)
+        for h in range(HALVES):
+            f_ps = bank(6 + h, "f_ps%d" % h)
+            for g in range(G_X):
+                mx(f_ps, x_codes, x_plane, wf_codes, wf_plane, g, g, BLK * h, g == 0, g == G_X - 1)
+            nc.vector.scalar_tensor_tensor(
+                out=fin[h][:], in0=f_ps[:], scalar=mask2[:, 0:1], in1=fin[h][:], op0=ALU.mult, op1=ALU.add
+            )
+        for j in range(N_BLK):
+            nc.vector.tensor_tensor(out=add[j][:], in0=add[j][:], in1=fin[j % HALVES][:], op=ALU.add)
+        sweep(0, acc_a, 7, G_H)
+
+        sums = [keep.tile([P, BLK], F32, name="sum%d" % h) for h in range(HALVES)]
+        gates = {}
+        prods = {}
+
+        def gate(j, acc, c0, c1):
+            z = work.tile([P, BLK], F32, name="z%d_%d" % (j, c0), tag="z")
+            nc.vector.tensor_tensor(out=z[:, 0 : c1 - c0], in0=acc[:, c0:c1], in1=add[j][:, c0:c1], op=ALU.add)
+            nc.scalar.activation(out=z[:, 0 : c1 - c0], in_=z[:, 0 : c1 - c0], func=ACT.Sigmoid)
+            gates[j, c0] = z
+
+        def product(j, c0, c1):
+            if j < HALVES:
+                p = sums[j][:, c0:c1]
+            else:
+                p_tile = work.tile([P, BLK], F32, name="p%d_%d" % (j, c0), tag="p")
+                p = p_tile[:, 0 : c1 - c0]
+            nc.vector.tensor_tensor(
+                out=p, in0=gates[j, c0][:, 0 : c1 - c0], in1=c_in[:, BLK * j + c0 : BLK * j + c1], op=ALU.mult
+            )
+            prods[j, c0] = p
+
+        def total(j, c0, c1):
+            if j >= HALVES:
+                s = sums[j % HALVES][:, c0:c1]
+                nc.vector.tensor_tensor(out=s, in0=s, in1=prods[j, c0], op=ALU.add)
+
+        def epilogue(items):
+            n = len(items)
+            for i in range(n + 2):
+                if i < n:
+                    gate(*items[i])
+                if 1 <= i <= n:
+                    j, acc, c0, c1 = items[i - 1]
+                    product(j, c0, c1)
+                if i >= 2:
+                    j, acc, c0, c1 = items[i - 2]
+                    total(j, c0, c1)
+
+        epilogue([(j, acc_a[j], 0, BLK) for j in range(SWEEPS[0])])
+        acc_b = [bank(b, "acc_b%d" % b) for b in (6, 7, 0)]
+        sweep(1, acc_b, 0, G_H)
+        epilogue([(SWEEPS[0] + i, acc_b[i], 0, BLK) for i in range(SWEEPS[1])])
+        nc.gpsimd.dma_start(out=out[:, 0:BLK], in_=sums[0][:])
+        acc_c = [bank(1, "acc_c")]
+        sweep(2, acc_c, 0, G_H)
+        last = N_BLK - 1
+        epilogue([(last, acc_c[0], c, c + BLK // 2) for c in (0, BLK // 2)])
+        nc.sync.dma_start(out=out[:, BLK : BLK + BLK // 2], in_=sums[1][:, 0 : BLK // 2])
+        nc.scalar.dma_start(out=out[:, BLK + BLK // 2 : H], in_=sums[1][:, BLK // 2 : BLK])

@@ -14,8 +14,9 @@ G_H = K // K_PASS
 G_X = X // K_PASS
 HALVES = H // BLK
 N_BLK = K // BLK
-SWEEPS = (6, 3, 1)
-PLANE_CUTS = ((0, 2, 5, 10), (0, 10), (0, 10))
+SWEEPS = (4, 3, 2, 1)
+PLANE_CUTS = ((0, 5, 10), (0, 10), (0, 10), (0, 10))
+CODE_CUTS = ((0, 2, 4, 6, 8, 10), (0, 3, 6, 8, 10), (0, 4, 8, 10), (0, 5, 8, 9, 10))
 
 F32 = mybir.dt.float32
 BF16 = mybir.dt.bfloat16
@@ -100,82 +101,36 @@ def tile_treelstmcell_pa_kernel(
         def w_load(s, g0, g1):
             load_codes(w_codes[s], W_aggr_f_words, g0, g1, sweep_col[s], BLK * SWEEPS[s])
 
-        def w_scale(s, i, r):
-            g0, g1, plane = w_plane[s][i]
-            rows_by_r(plane, W_aggr_f_scales, g0, g1, sweep_col[s], BLK * SWEEPS[s], r)
+        first = [(plane, W_aggr_f_scales, g0, g1, 0, BLK * SWEEPS[0]) for g0, g1, plane in w_plane[0]]
+        later = [
+            (plane, W_aggr_f_scales, g0, g1, sweep_col[s], BLK * SWEEPS[s])
+            for s in range(1, len(SWEEPS))
+            for g0, g1, plane in w_plane[s]
+        ]
+        planes = first + [(hf_plane, neighbour_h_scales, 0, G_H, 0, N)] + later[:1]
+        planes += [(x_plane, x_scales, 0, G_X, 0, N), (wf_plane, W_f_in_scales, 0, G_X, 0, H)] + later[1:]
+        for plane in planes:
+            zero(plane[0])
 
-        zero(hf_plane)
-        for g0, g1, plane in w_plane[0]:
-            zero(plane)
-        zero(x_plane)
-        zero(wf_plane)
-        zero(w_plane[1][0][2])
-        zero(w_plane[2][0][2])
+        chunks = [(s, g0, g1) for s, cuts in enumerate(CODE_CUTS) for g0, g1 in zip(cuts, cuts[1:])]
+        c_in = keep.tile([P, K - BLK], BF16, name="c_in")
+        c_last = keep.tile([P, BLK], BF16, name="c_last")
+        c_rows = neighbour_c.rearrange("n c h -> n (c h)")
 
-        def rows_of_quadrant(tile, scales, g0, g1, c0, cols, q):
-            nc.sync.dma_start(
-                out=tile[32 * q : 32 * q + 4, :, :].bitcast(I32),
-                in_=scales[g0:g1, 4 * q : 4 * q + 4, c0 : c0 + cols].rearrange("g q n -> q g n").bitcast(I32),
-            )
-
-        def x_rows(q):
-            rows_of_quadrant(x_plane, x_scales, 0, G_X, 0, N, q)
-
-        def wf_rows(q):
-            rows_of_quadrant(wf_plane, W_f_in_scales, 0, G_X, 0, H, q)
-
-        w_load(0, 0, 1)
+        w_load(*chunks[0])
         load_codes(hf_codes, neighbour_h_words, 0, G_H, 0, N)
-        for q in range(4):
-            rows_of_quadrant(hf_plane, neighbour_h_scales, 0, G_H, 0, N, q)
-        for q in range(4):
-            rows_of_quadrant(w_plane[0][0][2], W_aggr_f_scales, 0, 2, 0, BLK * SWEEPS[0], q)
-        w_load(0, 1, 2)
-        w_scale(0, 1, 0)
-        w_load(0, 2, 3)
-        w_scale(0, 1, 1)
-        w_load(0, 3, 4)
-        w_scale(0, 1, 2)
-        w_load(0, 4, 5)
-        w_scale(0, 1, 3)
+        w_load(*chunks[1])
+        for r in range(4):
+            for plane in planes:
+                rows_by_r(*plane, r)
         load_codes(x_codes, x_words, 0, G_X, 0, N)
         load_codes(wf_codes, W_f_in_words, 0, G_X, 0, H)
-        x_rows(0)
-        x_rows(1)
-        w_load(0, 5, 6)
-        w_scale(0, 2, 0)
-        x_rows(2)
-        x_rows(3)
-        w_load(0, 6, 7)
-        w_scale(0, 2, 1)
-        wf_rows(0)
-        wf_rows(1)
-        w_load(0, 7, 8)
-        w_scale(0, 2, 2)
-        wf_rows(2)
-        wf_rows(3)
-        w_load(0, 8, 9)
-        w_scale(0, 2, 3)
-        c_in = keep.tile([P, K], BF16, name="c_in")
-        nc.sync.dma_start(out=c_in[:], in_=neighbour_c.rearrange("n c h -> n (c h)"))
-        w_scale(1, 0, 0)
-        w_load(0, 9, 10)
-        w_scale(1, 0, 1)
-        w_load(1, 0, 2)
-        w_scale(1, 0, 2)
-        w_load(1, 2, 4)
-        w_scale(1, 0, 3)
-        w_load(1, 4, 6)
-        w_scale(2, 0, 0)
-        w_load(1, 6, 8)
-        w_scale(2, 0, 1)
-        w_load(1, 8, 10)
-        w_scale(2, 0, 2)
-        w_load(2, 0, 5)
-        w_scale(2, 0, 3)
-        w_load(2, 5, 8)
-        w_load(2, 8, 9)
-        w_load(2, 9, 10)
+        for chunk in chunks[2:4]:
+            w_load(*chunk)
+        nc.sync.dma_start(out=c_in[:], in_=c_rows[:, 0 : K - BLK])
+        for chunk in chunks[4:]:
+            w_load(*chunk)
+        nc.sync.dma_start(out=c_last[:], in_=c_rows[:, K - BLK : K])
 
         def mx(acc, a_codes, a_plane, b_codes, b_plane, b_g, g, n0, first, last):
             nc.tensor.matmul_mx(
@@ -193,10 +148,10 @@ def tile_treelstmcell_pa_kernel(
                 if g0 <= g < g1:
                     mx(acc, hf_codes, hf_plane, w_codes[s], plane, g - g0, g, BLK * i, g == 0, g == G_H - 1)
 
-        def sweep(s, accs, g0, g1, i0=0):
+        def sweep(s, accs, g0, g1):
             for g in range(g0, g1):
                 for i, acc in enumerate(accs):
-                    w_pass(s, g, i0 + i, acc)
+                    w_pass(s, g, i, acc)
 
         mask2 = keep.tile([P, 1], F32, name="mask2")
         fin = [keep.tile([P, BLK], F32, name="fin%d" % h) for h in range(HALVES)]
@@ -211,24 +166,20 @@ def tile_treelstmcell_pa_kernel(
                 nc.scalar.activation(out=fin[j - N_BLK][:], in_=acc[:], func=ACT.Copy, scale=mask2[:, 0:1])
 
         def spread_mask():
-            mask_ps = bank(6, "mask_ps")
+            mask_ps = bank(4, "mask_ps")
             nc.tensor.matmul(
                 out=mask_ps[:, 0:1], lhsT=rows[:, 0:N], rhs=ident[:, N_BLK + HALVES : N_BLK + HALVES + 1], start=True, stop=True
             )
             nc.scalar.mul(mask2[:], mask_ps[:, 0:1], 2.0)
 
-        acc_a = [bank(i, "acc_a%d" % i) for i in range(SWEEPS[0])]
-        sweep(0, acc_a, 0, 1)
         spread_mask()
-        spread(N_BLK, 7)
-        sweep(0, acc_a[0:3], 1, 2)
-        spread(N_BLK + 1, 6)
-        sweep(0, acc_a[3:], 1, 2, 3)
-        for g in range(2, 7):
-            sweep(0, acc_a[0:3], g, g + 1)
-            spread(2 * (g - 2), 7)
-            sweep(0, acc_a[3:], g, g + 1, 3)
-            spread(2 * (g - 2) + 1, 6)
+        for i in range(HALVES):
+            spread(N_BLK + i, 5 + i)
+        for j in range(N_BLK):
+            spread(j, 4 + (j + 3) % 4)
+
+        acc_a = [bank(i, "acc_a%d" % i) for i in range(SWEEPS[0])]
+        sweep(0, acc_a, 0, 4)
         for h in range(HALVES):
             f_ps = bank(6 + h, "f_ps%d" % h)
             for g in range(G_X):
@@ -238,17 +189,22 @@ def tile_treelstmcell_pa_kernel(
             )
         for j in range(N_BLK):
             nc.vector.tensor_tensor(out=add[j][:], in0=add[j][:], in1=fin[j % HALVES][:], op=ALU.add)
-        sweep(0, acc_a, 7, G_H)
+        sweep(0, acc_a, 4, G_H)
 
         sums = [keep.tile([P, BLK], F32, name="sum%d" % h) for h in range(HALVES)]
         gates = {}
         prods = {}
 
         def gate(j, acc, c0, c1):
-            z = work.tile([P, BLK], F32, name="z%d_%d" % (j, c0), tag="z")
+            z = work.tile([P, BLK], F32, name="z%d_%d" % (j, c0), tag="z", bufs=4)
             nc.vector.tensor_tensor(out=z[:, 0 : c1 - c0], in0=acc[:, c0:c1], in1=add[j][:, c0:c1], op=ALU.add)
             nc.scalar.activation(out=z[:, 0 : c1 - c0], in_=z[:, 0 : c1 - c0], func=ACT.Sigmoid)
             gates[j, c0] = z
+
+        def c_of(j, c0, c1):
+            if j == N_BLK - 1:
+                return c_last[:, c0:c1]
+            return c_in[:, BLK * j + c0 : BLK * j + c1]
 
         def product(j, c0, c1):
             if j < HALVES:
@@ -257,7 +213,7 @@ def tile_treelstmcell_pa_kernel(
                 p_tile = work.tile([P, BLK], F32, name="p%d_%d" % (j, c0), tag="p")
                 p = p_tile[:, 0 : c1 - c0]
             nc.vector.tensor_tensor(
-                out=p, in0=gates[j, c0][:, 0 : c1 - c0], in1=c_in[:, BLK * j + c0 : BLK * j + c1], op=ALU.mult
+                out=p, in0=gates[j, c0][:, 0 : c1 - c0], in1=c_of(j, c0, c1), op=ALU.mult
             )
             prods[j, c0] = p
 
@@ -279,13 +235,27 @@ def tile_treelstmcell_pa_kernel(
                     total(j, c0, c1)
 
         epilogue([(j, acc_a[j], 0, BLK) for j in range(SWEEPS[0])])
-        acc_b = [bank(b, "acc_b%d" % b) for b in (6, 7, 0)]
+        acc_b = [bank(4 + i, "acc_b%d" % i) for i in range(SWEEPS[1])]
         sweep(1, acc_b, 0, G_H)
         epilogue([(SWEEPS[0] + i, acc_b[i], 0, BLK) for i in range(SWEEPS[1])])
-        nc.gpsimd.dma_start(out=out[:, 0:BLK], in_=sums[0][:])
-        acc_c = [bank(1, "acc_c")]
+        acc_c = [bank(b, "acc_c%d" % b) for b in (7, 0)]
         sweep(2, acc_c, 0, G_H)
-        last = N_BLK - 1
-        epilogue([(last, acc_c[0], c, c + BLK // 2) for c in (0, BLK // 2)])
-        nc.sync.dma_start(out=out[:, BLK : BLK + BLK // 2], in_=sums[1][:, 0 : BLK // 2])
-        nc.scalar.dma_start(out=out[:, BLK + BLK // 2 : H], in_=sums[1][:, BLK // 2 : BLK])
+        acc_d = bank(1, "acc_d")
+        sweep(3, [acc_d], 0, G_H)
+        j = N_BLK - 3
+        half = BLK // 2
+        gate(j, acc_c[0], 0, BLK)
+        gate(j + 1, acc_c[1], 0, BLK)
+        product(j, 0, BLK)
+        product(j + 1, 0, BLK)
+        total(j, 0, BLK)
+        gate(j + 2, acc_d, 0, half)
+        gate(j + 2, acc_d, half, BLK)
+        total(j + 1, 0, BLK)
+        nc.sync.dma_start(out=out[:, 0:BLK], in_=sums[0][:])
+        product(j + 2, 0, half)
+        product(j + 2, half, BLK)
+        total(j + 2, 0, half)
+        nc.sync.dma_start(out=out[:, BLK : BLK + half], in_=sums[1][:, 0:half])
+        total(j + 2, half, BLK)
+        nc.scalar.dma_start(out=out[:, BLK + half : H], in_=sums[1][:, half:BLK])

from contextlib import ExitStack

import concourse.mybir as mybir
from concourse.masks import make_identity

N, N_CH, X, H = 128, 5, 1024, 1024
K = N_CH * H
FLOPS = 2 * N * (K * K + X * H)

P = 128
BLK = 512
K_PASS = 512
G_H = K // K_PASS
G_X = X // K_PASS
HALVES = H // BLK
N_BLK = K // BLK
SWEEPS = (4, 3, 2, 1)
PLANE_CUTS = ((0, 5, 10), (0, 10), (0, 10), (0, 10))
CODE_CUTS = ((0, 2, 4, 6, 8, 10), (0, 3, 6, 8, 10), (0, 4, 8, 10), (0, 5, 8, 9, 10))

F32 = mybir.dt.float32
BF16 = mybir.dt.bfloat16
I32 = mybir.dt.int32
U8 = mybir.dt.uint8
FP4X4 = mybir.dt.float4_e2m1fn_x4
ACT = mybir.ActivationFunctionType
ALU = mybir.AluOpType


def tile_treelstmcell_pa_kernel(
    tc,
    x_words,
    x_scales,
    x_mask,
    neighbour_h_words,
    neighbour_h_scales,
    neighbour_c,
    W_f_in_words,
    W_f_in_scales,
    b_f_in,
    W_aggr_f_words,
    W_aggr_f_scales,
    b_aggr_f,
    out,
):
    nc = tc.nc
    with ExitStack() as ctx:
        keep = ctx.enter_context(tc.tile_pool(name="keep", bufs=1))
        work = ctx.enter_context(tc.tile_pool(name="work", bufs=3))
        psum = ctx.enter_context(tc.psum_pool(name="psum", bufs=1))
        ctx.enter_context(tc.manual_schedule())

        def codes_tile(name, passes, cols):
            return keep.tile([P, passes, 2 * cols], U8, name=name, align_bytes=64)

        def plane_tile(name, passes, cols):
            return keep.tile([P, passes, cols], U8, name=name, align_bytes=64)

        def bank(i, name):
            return psum.tile([P, BLK], F32, name=name, tag="bank%d" % i)

        hf_codes = codes_tile("hf_codes", G_H, N)
        hf_plane = plane_tile("hf_plane", G_H, N)
        x_codes = codes_tile("x_codes", G_X, N)
        x_plane = plane_tile("x_plane", G_X, N)
        wf_codes = codes_tile("wf_codes", G_X, H)
        wf_plane = plane_tile("wf_plane", G_X, H)
        w_codes = [codes_tile("w_codes%d" % s, G_H, BLK * n) for s, n in enumerate(SWEEPS)]
        w_plane = [
            [(g0, g1, plane_tile("w_plane%d_%d" % (s, g0), g1 - g0, BLK * n)) for g0, g1 in zip(cuts, cuts[1:])]
            for s, (n, cuts) in enumerate(zip(SWEEPS, PLANE_CUTS))
        ]
        sweep_col = [BLK * sum(SWEEPS[:s]) for s in range(len(SWEEPS))]

        warm = keep.tile([P, 1], F32, name="warm")
        nc.gpsimd.memset(warm[:], 0.0)
        nc.scalar.activation(out=warm[:], in_=warm[:], func=ACT.Sigmoid)
        rows = keep.tile([P, BLK], BF16, name="rows")
        nc.gpsimd.memset(rows[:], 0.0)
        ident = keep.tile([P, P], BF16, name="ident")
        make_identity(nc, ident[:])
        nc.gpsimd.dma_start(out=rows[0:N_BLK, :], in_=b_aggr_f.rearrange("(j n) -> j n", n=BLK))
        nc.gpsimd.dma_start(out=rows[N_BLK : N_BLK + HALVES, :], in_=b_f_in.rearrange("(j n) -> j n", n=BLK))
        nc.gpsimd.dma_start(out=rows[N_BLK + HALVES : N_BLK + HALVES + 1, 0:N], in_=x_mask.unsqueeze(0))

        def zero(plane):
            nc.vector.memset(plane[:].rearrange("p g n -> p (g n)").bitcast(I32), 0)

        def load_codes(tile, words, g0, g1, c0, cols):
            nc.sync.dma_start(
                out=tile[:, g0:g1, :].bitcast(I32),
                in_=words[g0:g1, :, 2 * c0 : 2 * (c0 + cols)].rearrange("g p c -> p g c").bitcast(I32),
            )

        def rows_by_r(tile, scales, g0, g1, c0, cols, r):
            nc.sync.dma_start(
                out=tile[r:P:32, :, :].bitcast(I32),
                in_=scales[g0:g1, r:16:4, c0 : c0 + cols].rearrange("g q n -> q g n").bitcast(I32),
            )

        def w_load(s, g0, g1):
            load_codes(w_codes[s], W_aggr_f_words, g0, g1, sweep_col[s], BLK * SWEEPS[s])

        first = [(plane, W_aggr_f_scales, g0, g1, 0, BLK * SWEEPS[0]) for g0, g1, plane in w_plane[0]]
        later = [
            (plane, W_aggr_f_scales, g0, g1, sweep_col[s], BLK * SWEEPS[s])
            for s in range(1, len(SWEEPS))
            for g0, g1, plane in w_plane[s]
        ]
        planes = first + [(hf_plane, neighbour_h_scales, 0, G_H, 0, N)] + later[:1]
        planes += [(x_plane, x_scales, 0, G_X, 0, N), (wf_plane, W_f_in_scales, 0, G_X, 0, H)] + later[1:]
        for plane in planes:
            zero(plane[0])

        chunks = [(s, g0, g1) for s, cuts in enumerate(CODE_CUTS) for g0, g1 in zip(cuts, cuts[1:])]
        c_in = keep.tile([P, K - BLK], BF16, name="c_in")
        c_last = keep.tile([P, BLK], BF16, name="c_last")
        c_rows = neighbour_c.rearrange("n c h -> n (c h)")

        w_load(*chunks[0])
        load_codes(hf_codes, neighbour_h_words, 0, G_H, 0, N)
        w_load(*chunks[1])
        for r in range(4):
            for plane in planes:
                rows_by_r(*plane, r)
        load_codes(x_codes, x_words, 0, G_X, 0, N)
        load_codes(wf_codes, W_f_in_words, 0, G_X, 0, H)
        for chunk in chunks[2:4]:
            w_load(*chunk)
        nc.sync.dma_start(out=c_in[:], in_=c_rows[:, 0 : K - BLK])
        for chunk in chunks[4:]:
            w_load(*chunk)
        nc.sync.dma_start(out=c_last[:], in_=c_rows[:, K - BLK : K])

        def mx(acc, a_codes, a_plane, b_codes, b_plane, b_g, g, n0, first, last):
            nc.tensor.matmul_mx(
                out=acc[:],
                lhsT=a_codes[:, g, :].bitcast(FP4X4),
                lhsT_scale=a_plane[:, g, :],
                rhs=b_codes[:, g, 2 * n0 : 2 * (n0 + BLK)].bitcast(FP4X4),
                rhs_scale=b_plane[:, b_g, n0 : n0 + BLK],
                start=first,
                stop=last,
            )

        def w_pass(s, g, i, acc):
            for g0, g1, plane in w_plane[s]:
                if g0 <= g < g1:
                    mx(acc, hf_codes, hf_plane, w_codes[s], plane, g - g0, g, BLK * i, g == 0, g == G_H - 1)

        def sweep(s, accs, g0, g1):
            for g in range(g0, g1):
                for i, acc in enumerate(accs):
                    w_pass(s, g, i, acc)

        mask2 = keep.tile([P, 1], F32, name="mask2")
        fin = [keep.tile([P, BLK], F32, name="fin%d" % h) for h in range(HALVES)]
        add = [keep.tile([P, BLK], F32, name="add%d" % j) for j in range(N_BLK)]

        def spread(j, b):
            acc = bank(b, "bias_ps%d" % j)
            nc.tensor.matmul(out=acc[:], lhsT=ident[:, j : j + 1].to_broadcast([P, P]), rhs=rows[:], start=True, stop=True)
            if j < N_BLK:
                nc.scalar.copy(out=add[j][:], in_=acc[:])
            else:
                nc.scalar.activation(out=fin[j - N_BLK][:], in_=acc[:], func=ACT.Copy, scale=mask2[:, 0:1])

        def spread_mask():
            mask_ps = bank(4, "mask_ps")
            nc.tensor.matmul(
                out=mask_ps[:, 0:1], lhsT=rows[:, 0:N], rhs=ident[:, N_BLK + HALVES : N_BLK + HALVES + 1], start=True, stop=True
            )
            nc.scalar.mul(mask2[:], mask_ps[:, 0:1], 2.0)

        spread_mask()
        for i in range(HALVES):
            spread(N_BLK + i, 5 + i)
        for j in range(N_BLK):
            spread(j, 4 + (j + 3) % 4)

        acc_a = [bank(i, "acc_a%d" % i) for i in range(SWEEPS[0])]
        sweep(0, acc_a, 0, 4)
        for h in range(HALVES):
            f_ps = bank(6 + h, "f_ps%d" % h)
            for g in range(G_X):
                mx(f_ps, x_codes, x_plane, wf_codes, wf_plane, g, g, BLK * h, g == 0, g == G_X - 1)
            nc.vector.scalar_tensor_tensor(
                out=fin[h][:], in0=f_ps[:], scalar=mask2[:, 0:1], in1=fin[h][:], op0=ALU.mult, op1=ALU.add
            )
        for j in range(N_BLK):
            nc.vector.tensor_tensor(out=add[j][:], in0=add[j][:], in1=fin[j % HALVES][:], op=ALU.add)
        sweep(0, acc_a, 4, G_H)

        sums = [keep.tile([P, BLK], F32, name="sum%d" % h) for h in range(HALVES)]
        gates = {}
        prods = {}

        def gate(j, acc, c0, c1):
            z = work.tile([P, BLK], F32, name="z%d_%d" % (j, c0), tag="z", bufs=4)
            nc.vector.tensor_tensor(out=z[:, 0 : c1 - c0], in0=acc[:, c0:c1], in1=add[j][:, c0:c1], op=ALU.add)
            nc.scalar.activation(out=z[:, 0 : c1 - c0], in_=z[:, 0 : c1 - c0], func=ACT.Sigmoid)
            gates[j, c0] = z

        def c_of(j, c0, c1):
            if j == N_BLK - 1:
                return c_last[:, c0:c1]
            return c_in[:, BLK * j + c0 : BLK * j + c1]

        def product(j, c0, c1):
            if j < HALVES:
                p = sums[j][:, c0:c1]
            else:
                p_tile = work.tile([P, BLK], F32, name="p%d_%d" % (j, c0), tag="p")
                p = p_tile[:, 0 : c1 - c0]
            nc.vector.tensor_tensor(
                out=p, in0=gates[j, c0][:, 0 : c1 - c0], in1=c_of(j, c0, c1), op=ALU.mult
            )
            prods[j, c0] = p

        def total(j, c0, c1):
            if j >= HALVES:
                s = sums[j % HALVES][:, c0:c1]
                nc.vector.tensor_tensor(out=s, in0=s, in1=prods[j, c0], op=ALU.add)

        def epilogue(items):
            n = len(items)
            for i in range(n + 2):
                if i < n:
                    gate(*items[i])
                if 1 <= i <= n:
                    j, acc, c0, c1 = items[i - 1]
                    product(j, c0, c1)
                if i >= 2:
                    j, acc, c0, c1 = items[i - 2]
                    total(j, c0, c1)

        epilogue([(j, acc_a[j], 0, BLK) for j in range(SWEEPS[0])])
        acc_b = [bank(4 + i, "acc_b%d" % i) for i in range(SWEEPS[1])]
        sweep(1, acc_b, 0, G_H)
        epilogue([(SWEEPS[0] + i, acc_b[i], 0, BLK) for i in range(SWEEPS[1])])
        acc_c = [bank(b, "acc_c%d" % b) for b in (7, 0)]
        sweep(2, acc_c, 0, G_H)
        acc_d = bank(1, "acc_d")
        sweep(3, [acc_d], 0, G_H)
        j = N_BLK - 3
        half = BLK // 2
        gate(j, acc_c[0], 0, BLK)
        gate(j + 1, acc_c[1], 0, BLK)
        product(j, 0, BLK)
        product(j + 1, 0, BLK)
        total(j, 0, BLK)
        gate(j + 2, acc_d, 0, half)
        gate(j + 2, acc_d, half, BLK)
        total(j + 1, 0, BLK)
        nc.sync.dma_start(out=out[:, 0:BLK], in_=sums[0][:])
        product(j + 2, 0, half)
        product(j + 2, half, BLK)
        total(j + 2, 0, half)
        nc.sync.dma_start(out=out[:, BLK : BLK + half], in_=sums[1][:, 0:half])
        total(j + 2, half, BLK)
        nc.scalar.dma_start(out=out[:, BLK + half : H], in_=sums[1][:, half:BLK])
